import numpy as np
import ml_dtypes


def mxq(x, axis, fmt="e4m3"):
    dtype, down = {"e4m3": (ml_dtypes.float8_e4m3fn, 7), "e5m2": (ml_dtypes.float8_e5m2, 14)}[fmt]
    v = np.moveaxis(np.asarray(x, np.float32).astype(ml_dtypes.bfloat16).astype(np.float64), axis, -1)
    blocks = v.reshape(v.shape[:-1] + (-1, 32))
    amax = np.abs(blocks).max(-1, keepdims=True)
    byte = np.maximum(np.where(amax > 0, np.frexp(amax)[1] - 1 + 127, 0) - down, 1)
    scale = np.exp2(byte - 127.0)
    codes = (blocks / scale).astype(np.float32).astype(dtype).astype(np.float64)
    return np.moveaxis((codes * scale).reshape(v.shape), -1, axis)


BF16 = ml_dtypes.bfloat16


def bf(x):
    return np.asarray(x, np.float32).astype(BF16)


def f64(x):
    return np.asarray(x).astype(np.float64)


B, D, C = 256, 16384, 512
REACH_SCALE = 10.0
COS_SCALE = 16.0


def setup_inputs():
    return {"x": bf(np.random.standard_normal((B, D))),
            "infused_feature": bf(np.random.standard_normal((B, D)) * 0.2),
            "min_dist": bf(np.sqrt(2.0 * D) * np.random.uniform(0.7, 1.2, (B, 1))),
            "W_cos": bf(np.random.standard_normal((C, D)) * np.random.uniform(0.5, 1.5, (C, 1)) / np.sqrt(D))}


def reference(x, infused_feature, min_dist, W_cos):
    reachability = REACH_SCALE / f64(min_dist)
    feat = reachability * (f64(x) + f64(infused_feature))
    norm_x = np.sqrt((feat * feat).sum(1, keepdims=True))
    ex = (norm_x / (1.0 + norm_x)) * (feat / norm_x)
    w = f64(W_cos)
    ew = w / np.sqrt((w * w).sum(1, keepdims=True))
    return mxq(COS_SCALE * ex, 1, "e4m3") @ mxq(ew, 1, "e4m3").T

@@ -1,0 +1,267 @@
+from contextlib import ExitStack
+
+import concourse.mybir as mybir
+from concourse.masks import make_identity
+
+F32 = mybir.dt.float32
+BF16 = mybir.dt.bfloat16
+U32 = mybir.dt.uint32
+U8 = mybir.dt.uint8
+FP8X4 = mybir.dt.float8_e4m3fn_x4
+ACT = mybir.ActivationFunctionType
+ALU = mybir.AluOpType
+AXIS = mybir.AxisListType
+
+B, D, C = 256, 16384, 512
+REACH_SCALE = 10.0
+COS_SCALE = 16.0
+FLOPS = 2 * B * C * D
+
+P = 128
+X_TILES = B // P
+W_TILES = C // P
+TILES = X_TILES + W_TILES
+
+K_PASS = 4 * P
+PASSES = D // K_PASS
+CHUNK = 2048
+CHUNKS = D // CHUNK
+STEPS = TILES * CHUNKS
+CHUNK_PASSES = CHUNK // K_PASS
+CHUNK_CODES = CHUNK // 4
+BANK_WORDS = 512
+BANK_BLOCKS = BANK_WORDS // P
+CHUNK_BANKS = CHUNK // 2 // BANK_WORDS
+
+SLOT_BYTES = 2 * D
+HALF_CHUNKS = SLOT_BYTES // (4 * CHUNK)
+RING_SLOTS = 4
+
+AHEAD = 2
+LEAD = 2
+
+
+def tile_metaembedding_classifier_pb_k_kernel(
+    tc, x, infused_feature, min_dist, W_cos, out
+):
+    nc = tc.nc
+    with ExitStack() as ctx:
+        ctx.enter_context(tc.manual_schedule())
+        keep = ctx.enter_context(tc.tile_pool(name="keep", bufs=1))
+        ring = ctx.enter_context(tc.tile_pool(name="ring", bufs=RING_SLOTS))
+        stream = ctx.enter_context(tc.tile_pool(name="stream", bufs=3))
+        psum = ctx.enter_context(tc.psum_pool(name="psum", bufs=1))
+
+        identity = keep.tile([P, P], F32)
+        make_identity(nc, identity[:])
+
+        one = keep.tile([P, 1], F32)
+        nc.vector.memset(one[:], 1.0)
+        warm = keep.tile([P, 1], F32)
+        nc.scalar.activation(out=warm[:], in_=one[:], func=ACT.Sqrt)
+
+        distance = {}
+        for t in range(X_TILES):
+            dist = keep.tile([P, 1], BF16, name="dist%d" % t)
+            nc.scalar.dma_start(out=dist[:], in_=min_dist[t * P : (t + 1) * P, :])
+            distance[t] = dist
+
+        x_codes = keep.tile([P, X_TILES * PASSES * P], U32, align_bytes=64)
+        x_scales = keep.tile([P, X_TILES * PASSES * P], U8, align_bytes=64)
+        squares = keep.tile([P, CHUNK], BF16)
+
+        raw = {}
+        slots = {}
+        partial = {}
+        roots = {}
+        factors = {}
+        banks = {}
+        grouped = {}
+        w_operand = {}
+        sums = {}
+
+        def source(t, j):
+            if t < X_TILES:
+                i = j % HALF_CHUNKS
+                return slots[(t, j // HALF_CHUNKS)][:, i * CHUNK : (i + 1) * CHUNK]
+            return slots[(t, 0)][:, j * CHUNK : (j + 1) * CHUNK]
+
+        def load(h):
+            t, j = divmod(h, CHUNKS)
+            cols = slice(j * CHUNK, (j + 1) * CHUNK)
+            if t < X_TILES:
+                rows = slice(t * P, (t + 1) * P)
+                direct = stream.tile([P, CHUNK], BF16, tag="direct")
+                nc.sync.dma_start(out=direct[:], in_=x[rows, cols])
+                infused = stream.tile([P, CHUNK], BF16, tag="infused")
+                nc.sync.dma_start(out=infused[:], in_=infused_feature[rows, cols])
+                raw[h] = (direct, infused)
+            else:
+                rows = slice((t - X_TILES) * P, (t - X_TILES + 1) * P)
+                if j == 0:
+                    weights = ring.tile([P, D], BF16, tag="slot")
+                    slots[(t, 0)] = weights
+                nc.sync.dma_start(out=source(t, j), in_=W_cos[rows, cols])
+
+        def sum_squares(h):
+            t, j = divmod(h, CHUNKS)
+            if j == 0:
+                parts = keep.tile([P, CHUNKS], F32, name="parts%d" % t)
+                partial[t] = parts
+            if t < X_TILES:
+                if j % HALF_CHUNKS == 0:
+                    fused = ring.tile([P, HALF_CHUNKS * CHUNK], F32, tag="slot")
+                    slots[(t, j // HALF_CHUNKS)] = fused
+                direct, infused = raw[h]
+                nc.vector.tensor_tensor(
+                    out=source(t, j), in0=direct[:], in1=infused[:], op=ALU.add
+                )
+            nc.scalar.activation(
+                out=squares[:],
+                in_=source(t, j),
+                func=ACT.Square,
+                accum_out=partial[t][:, j : j + 1],
+            )
+
+        def norm(t):
+            total = keep.tile([P, 1], F32, name="total%d" % t)
+            nc.vector.reduce_sum(out=total[:], in_=partial[t][:], axis=AXIS.X)
+            root = keep.tile([P, 1], F32, name="root%d" % t)
+            nc.scalar.activation(out=root[:], in_=total[:], func=ACT.Sqrt)
+            roots[t] = root
+
+        def factor(t):
+            scale = keep.tile([P, 1], F32, name="scale%d" % t)
+            factors[t] = scale
+            if t >= X_TILES:
+                nc.vector.reciprocal(out=scale[:], in_=roots[t][:])
+                return
+            reach = keep.tile([P, 1], F32, name="reach%d" % t)
+            nc.vector.reciprocal(out=reach[:], in_=distance[t][:])
+            nc.vector.tensor_scalar(
+                out=reach[:], in0=reach[:], scalar1=REACH_SCALE, scalar2=None, op0=ALU.mult
+            )
+            shrink = keep.tile([P, 1], F32, name="shrink%d" % t)
+            nc.vector.tensor_scalar(
+                out=shrink[:],
+                in0=roots[t][:],
+                scalar1=reach[:, 0:1],
+                scalar2=1.0,
+                op0=ALU.mult,
+                op1=ALU.add,
+            )
+            nc.vector.reciprocal(out=shrink[:], in_=shrink[:])
+            nc.vector.tensor_scalar(
+                out=scale[:],
+                in0=shrink[:],
+                scalar1=reach[:, 0:1],
+                scalar2=COS_SCALE,
+                op0=ALU.mult,
+                op1=ALU.mult,
+            )
+
+        def scale_and_transpose(g):
+            t, j = divmod(g, CHUNKS)
+            scaled = stream.tile([P, CHUNK], BF16, tag="scaled")
+            nc.vector.tensor_scalar(
+                out=scaled[:],
+                in0=source(t, j),
+                scalar1=factors[t][:, 0:1],
+                scalar2=None,
+                op0=ALU.mult,
+            )
+            words = scaled[:].bitcast(F32)
+            banks[g] = []
+            for n in range(CHUNK_BANKS):
+                bank = psum.tile([P, BANK_WORDS], F32, tag="bank", bufs=6)
+                for b in range(BANK_BLOCKS):
+                    block = n * BANK_BLOCKS + b
+                    nc.tensor.transpose(
+                        out=bank[:, b * P : (b + 1) * P],
+                        in_=words[:, block * P : (block + 1) * P],
+                        identity=identity[:],
+                    )
+                banks[g].append(bank)
+
+        def empty_banks(g):
+            t = g // CHUNKS
+            ordered = stream.tile([P, CHUNK], BF16, tag="ordered", align_bytes=64)
+            grouped[g] = ordered
+            pairs = ordered[:].bitcast(F32)
+            for n in range(CHUNK_BANKS):
+                dst = pairs[:, n * BANK_WORDS : (n + 1) * BANK_WORDS].rearrange(
+                    "p (q r u) -> p q r u", r=P, u=2
+                )
+                src = banks[g][n][:].rearrange("p (q u r) -> p q r u", r=P, u=2)
+                if X_TILES <= t + 1 < TILES:
+                    nc.vector.tensor_copy(out=dst, in_=src)
+                else:
+                    nc.scalar.copy(out=dst, in_=src)
+
+        def quantise(g):
+            t, j = divmod(g, CHUNKS)
+            if t < X_TILES:
+                first = (t * PASSES + j * CHUNK_PASSES) * P
+                codes = x_codes[:, first : first + CHUNK_CODES]
+                scales = x_scales[:, first : first + CHUNK_CODES]
+            else:
+                w_codes = stream.tile([P, CHUNK_CODES], U32, tag="w_codes", align_bytes=64)
+                w_scales = stream.tile([P, CHUNK_CODES], U8, tag="w_scales", align_bytes=64)
+                w_operand[g] = (w_codes, w_scales)
+                codes = w_codes[:]
+                scales = w_scales[:]
+            nc.vector.quantize_mx(out=codes.bitcast(FP8X4), scales=scales, in_=grouped[g][:])
+
+        def multiply(g):
+            t, j = divmod(g, CHUNKS)
+            w_codes, w_scales = w_operand[g]
+            for s in range(X_TILES):
+                if j == 0:
+                    product = psum.tile([P, P], F32, tag="product", bufs=X_TILES)
+                    sums[(t, s)] = product
+                for q in range(CHUNK_PASSES):
+                    k_pass = j * CHUNK_PASSES + q
+                    x_cols = slice((s * PASSES + k_pass) * P, (s * PASSES + k_pass + 1) * P)
+                    w_cols = slice(q * P, (q + 1) * P)
+                    nc.tensor.matmul_mx(
+                        out=sums[(t, s)][:],
+                        lhsT=x_codes[:, x_cols].bitcast(FP8X4),
+                        lhsT_scale=x_scales[:, x_cols],
+                        rhs=w_codes[:, w_cols].bitcast(FP8X4),
+                        rhs_scale=w_scales[:, w_cols],
+                        start=(k_pass == 0),
+                        stop=(k_pass == PASSES - 1),
+                    )
+
+        def store(t):
+            cols = slice((t - X_TILES) * P, (t - X_TILES + 1) * P)
+            for s in range(X_TILES):
+                logits = stream.tile([P, P], F32, tag="logits")
+                if s % 2 == 0:
+                    nc.vector.tensor_copy(out=logits[:], in_=sums[(t, s)][:])
+                else:
+                    nc.scalar.copy(out=logits[:], in_=sums[(t, s)][:])
+                nc.sync.dma_start(out=out[s * P : (s + 1) * P, cols], in_=logits[:])
+
+        for h in range(AHEAD):
+            load(h)
+        for h in range(STEPS + CHUNKS + LEAD + 3):
+            g = h - CHUNKS - LEAD
+            if h + AHEAD < STEPS:
+                load(h + AHEAD)
+            if h < STEPS:
+                sum_squares(h)
+            if h % CHUNKS == 0 and 0 < h <= STEPS:
+                norm(h // CHUNKS - 1)
+            if h % CHUNKS == 1 and 1 < h <= STEPS + 1:
+                factor(h // CHUNKS - 1)
+            if 0 <= g < STEPS:
+                scale_and_transpose(g)
+            if 0 <= g - 1 < STEPS:
+                empty_banks(g - 1)
+            if 0 <= g - 2 < STEPS:
+                quantise(g - 2)
+            if (g - 3) % CHUNKS == CHUNKS - 1 and X_TILES * CHUNKS <= g - 3 < STEPS:
+                store((g - 3) // CHUNKS)
+            if X_TILES * CHUNKS <= g - 2 < STEPS:
+                multiply(g - 2)

@@ -38,6 +38,8 @@ HALF_CHUNKS = SLOT_BYTES // (4 * CHUNK)
 RING_SLOTS = 4
 
 AHEAD = 2
+SQUARED = 1
+RELIEF = 4
 LEAD = 2
 
 
@@ -68,7 +70,7 @@ def tile_metaembedding_classifier_pb_k_kernel(
 
         x_codes = keep.tile([P, X_TILES * PASSES * P], U32, align_bytes=64)
         x_scales = keep.tile([P, X_TILES * PASSES * P], U8, align_bytes=64)
-        squares = keep.tile([P, CHUNK], BF16)
+        squares = keep.tile([P, SQUARED * CHUNK], BF16)
 
         raw = {}
         slots = {}
@@ -80,11 +82,11 @@ def tile_metaembedding_classifier_pb_k_kernel(
         w_operand = {}
         sums = {}
 
-        def source(t, j):
+        def source(t, j, n=1):
             if t < X_TILES:
                 i = j % HALF_CHUNKS
-                return slots[(t, j // HALF_CHUNKS)][:, i * CHUNK : (i + 1) * CHUNK]
-            return slots[(t, 0)][:, j * CHUNK : (j + 1) * CHUNK]
+                return slots[(t, j // HALF_CHUNKS)][:, i * CHUNK : (i + n) * CHUNK]
+            return slots[(t, 0)][:, j * CHUNK : (j + n) * CHUNK]
 
         def load(h):
             t, j = divmod(h, CHUNKS)
@@ -106,7 +108,7 @@ def tile_metaembedding_classifier_pb_k_kernel(
         def sum_squares(h):
             t, j = divmod(h, CHUNKS)
             if j == 0:
-                parts = keep.tile([P, CHUNKS], F32, name="parts%d" % t)
+                parts = keep.tile([P, CHUNKS // SQUARED], F32, name="parts%d" % t)
                 partial[t] = parts
             if t < X_TILES:
                 if j % HALF_CHUNKS == 0:
@@ -116,12 +118,13 @@ def tile_metaembedding_classifier_pb_k_kernel(
                 nc.vector.tensor_tensor(
                     out=source(t, j), in0=direct[:], in1=infused[:], op=ALU.add
                 )
-            nc.scalar.activation(
-                out=squares[:],
-                in_=source(t, j),
-                func=ACT.Square,
-                accum_out=partial[t][:, j : j + 1],
-            )
+            if j % SQUARED == SQUARED - 1:
+                nc.scalar.activation(
+                    out=squares[:],
+                    in_=source(t, j - (SQUARED - 1), SQUARED),
+                    func=ACT.Square,
+                    accum_out=partial[t][:, j // SQUARED : j // SQUARED + 1],
+                )
 
         def norm(t):
             total = keep.tile([P, 1], F32, name="total%d" % t)
@@ -183,8 +186,7 @@ def tile_metaembedding_classifier_pb_k_kernel(
                     )
                 banks[g].append(bank)
 
-        def empty_banks(g):
-            t = g // CHUNKS
+        def empty_banks(g, by_vector):
             ordered = stream.tile([P, CHUNK], BF16, tag="ordered", align_bytes=64)
             grouped[g] = ordered
             pairs = ordered[:].bitcast(F32)
@@ -193,7 +195,7 @@ def tile_metaembedding_classifier_pb_k_kernel(
                     "p (q r u) -> p q r u", r=P, u=2
                 )
                 src = banks[g][n][:].rearrange("p (q u r) -> p q r u", r=P, u=2)
-                if X_TILES <= t + 1 < TILES:
+                if by_vector and not (n == 0 and g % RELIEF == 0):
                     nc.vector.tensor_copy(out=dst, in_=src)
                 else:
                     nc.scalar.copy(out=dst, in_=src)
@@ -258,7 +260,7 @@ def tile_metaembedding_classifier_pb_k_kernel(
             if 0 <= g < STEPS:
                 scale_and_transpose(g)
             if 0 <= g - 1 < STEPS:
-                empty_banks(g - 1)
+                empty_banks(g - 1, by_vector=(X_TILES * CHUNKS <= h < STEPS))
             if 0 <= g - 2 < STEPS:
                 quantise(g - 2)
             if (g - 3) % CHUNKS == CHUNKS - 1 and X_TILES * CHUNKS <= g - 3 < STEPS:

@@ -37,7 +37,7 @@ SLOT_BYTES = 2 * D
 HALF_CHUNKS = SLOT_BYTES // (4 * CHUNK)
 RING_SLOTS = 4
 
-AHEAD = 2
+AHEAD = 3
 SQUARED = 1
 RELIEF = 4
 LEAD = 2
@@ -93,9 +93,9 @@ def tile_metaembedding_classifier_pb_k_kernel(
             cols = slice(j * CHUNK, (j + 1) * CHUNK)
             if t < X_TILES:
                 rows = slice(t * P, (t + 1) * P)
-                direct = stream.tile([P, CHUNK], BF16, tag="direct")
+                direct = stream.tile([P, CHUNK], BF16, tag="direct", bufs=AHEAD + 1)
                 nc.sync.dma_start(out=direct[:], in_=x[rows, cols])
-                infused = stream.tile([P, CHUNK], BF16, tag="infused")
+                infused = stream.tile([P, CHUNK], BF16, tag="infused", bufs=AHEAD + 1)
                 nc.sync.dma_start(out=infused[:], in_=infused_feature[rows, cols])
                 raw[h] = (direct, infused)
             else:
@@ -165,7 +165,7 @@ def tile_metaembedding_classifier_pb_k_kernel(
 
         def scale_and_transpose(g):
             t, j = divmod(g, CHUNKS)
-            scaled = stream.tile([P, CHUNK], BF16, tag="scaled")
+            scaled = stream.tile([P, CHUNK], BF16, tag="scaled", bufs=2)
             nc.vector.tensor_scalar(
                 out=scaled[:],
                 in0=source(t, j),

@@ -20,26 +20,25 @@ FLOPS = 2 * B * C * D
 P = 128
 X_TILES = B // P
 W_TILES = C // P
-TILES = X_TILES + W_TILES
+
+SEQUENCE = (("w", 0), ("x", 0), ("w", 1), ("x", 1), ("w", 2), ("w", 3))
 
 K_PASS = 4 * P
 PASSES = D // K_PASS
 CHUNK = 2048
 CHUNKS = D // CHUNK
-STEPS = TILES * CHUNKS
+STEPS = len(SEQUENCE) * CHUNKS
 CHUNK_PASSES = CHUNK // K_PASS
 CHUNK_CODES = CHUNK // 4
 BANK_WORDS = 512
 BANK_BLOCKS = BANK_WORDS // P
 CHUNK_BANKS = CHUNK // 2 // BANK_WORDS
 
-SLOT_BYTES = 2 * D
-HALF_CHUNKS = SLOT_BYTES // (4 * CHUNK)
-RING_SLOTS = 4
+SLOT_BYTES = 4 * CHUNK
+W_SLOT_CHUNKS = 2
+RING_SLOTS = 12
 
-AHEAD = 3
-SQUARED = 1
-RELIEF = 4
+AHEAD = 2
 LEAD = 2
 
 
@@ -51,7 +50,7 @@ def tile_metaembedding_classifier_pb_k_kernel(
         ctx.enter_context(tc.manual_schedule())
         keep = ctx.enter_context(tc.tile_pool(name="keep", bufs=1))
         ring = ctx.enter_context(tc.tile_pool(name="ring", bufs=RING_SLOTS))
-        stream = ctx.enter_context(tc.tile_pool(name="stream", bufs=3))
+        stream = ctx.enter_context(tc.tile_pool(name="stream", bufs=2))
         psum = ctx.enter_context(tc.psum_pool(name="psum", bufs=1))
 
         identity = keep.tile([P, P], F32)
@@ -68,9 +67,12 @@ def tile_metaembedding_classifier_pb_k_kernel(
             nc.scalar.dma_start(out=dist[:], in_=min_dist[t * P : (t + 1) * P, :])
             distance[t] = dist
 
-        x_codes = keep.tile([P, X_TILES * PASSES * P], U32, align_bytes=64)
-        x_scales = keep.tile([P, X_TILES * PASSES * P], U8, align_bytes=64)
-        squares = keep.tile([P, SQUARED * CHUNK], BF16)
+        kept = {}
+        for kind, t in SEQUENCE[:4]:
+            codes = keep.tile([P, PASSES * P], U32, name="codes_%s%d" % (kind, t), align_bytes=64)
+            scales = keep.tile([P, PASSES * P], U8, name="scales_%s%d" % (kind, t), align_bytes=64)
+            kept[(kind, t)] = (codes, scales)
+        squares = keep.tile([P, CHUNK], BF16)
 
         raw = {}
         slots = {}
@@ -79,65 +81,80 @@ def tile_metaembedding_classifier_pb_k_kernel(
         factors = {}
         banks = {}
         grouped = {}
-        w_operand = {}
+        operand = {}
         sums = {}
 
-        def source(t, j, n=1):
-            if t < X_TILES:
-                i = j % HALF_CHUNKS
-                return slots[(t, j // HALF_CHUNKS)][:, i * CHUNK : (i + n) * CHUNK]
-            return slots[(t, 0)][:, j * CHUNK : (j + n) * CHUNK]
+        def kind_of(h):
+            return SEQUENCE[h // CHUNKS][0] if 0 <= h < STEPS else None
+
+        def source(h):
+            i, j = divmod(h, CHUNKS)
+            if SEQUENCE[i][0] == "x":
+                return slots[(i, j)][:]
+            c = (j % W_SLOT_CHUNKS) * CHUNK
+            return slots[(i, j // W_SLOT_CHUNKS)][:, c : c + CHUNK]
 
         def load(h):
-            t, j = divmod(h, CHUNKS)
+            i, j = divmod(h, CHUNKS)
+            kind, t = SEQUENCE[i]
+            rows = slice(t * P, (t + 1) * P)
             cols = slice(j * CHUNK, (j + 1) * CHUNK)
-            if t < X_TILES:
-                rows = slice(t * P, (t + 1) * P)
+            if kind == "x":
                 direct = stream.tile([P, CHUNK], BF16, tag="direct", bufs=AHEAD + 1)
                 nc.sync.dma_start(out=direct[:], in_=x[rows, cols])
                 infused = stream.tile([P, CHUNK], BF16, tag="infused", bufs=AHEAD + 1)
                 nc.sync.dma_start(out=infused[:], in_=infused_feature[rows, cols])
                 raw[h] = (direct, infused)
             else:
-                rows = slice((t - X_TILES) * P, (t - X_TILES + 1) * P)
-                if j == 0:
-                    weights = ring.tile([P, D], BF16, tag="slot")
-                    slots[(t, 0)] = weights
-                nc.sync.dma_start(out=source(t, j), in_=W_cos[rows, cols])
+                if j % W_SLOT_CHUNKS == 0:
+                    weights = ring.tile([P, W_SLOT_CHUNKS * CHUNK], BF16, tag="slot")
+                    slots[(i, j // W_SLOT_CHUNKS)] = weights
+                nc.sync.dma_start(out=source(h), in_=W_cos[rows, cols])
 
         def sum_squares(h):
-            t, j = divmod(h, CHUNKS)
+            i, j = divmod(h, CHUNKS)
             if j == 0:
-                parts = keep.tile([P, CHUNKS // SQUARED], F32, name="parts%d" % t)
-                partial[t] = parts
-            if t < X_TILES:
-                if j % HALF_CHUNKS == 0:
-                    fused = ring.tile([P, HALF_CHUNKS * CHUNK], F32, tag="slot")
-                    slots[(t, j // HALF_CHUNKS)] = fused
+                parts = keep.tile([P, CHUNKS], F32, name="parts%d" % i)
+                partial[i] = parts
+            if SEQUENCE[i][0] == "x":
+                fused = ring.tile([P, CHUNK], F32, tag="slot")
+                slots[(i, j)] = fused
                 direct, infused = raw[h]
                 nc.vector.tensor_tensor(
-                    out=source(t, j), in0=direct[:], in1=infused[:], op=ALU.add
+                    out=fused[:], in0=direct[:], in1=infused[:], op=ALU.add
                 )
-            if j % SQUARED == SQUARED - 1:
+            if i == 0 and j % 2 == 1:
+                unread = stream.tile([P, CHUNK], BF16, tag="scaled")
+                nc.vector.scalar_tensor_tensor(
+                    out=unread[:],
+                    in0=source(h),
+                    scalar=1.0,
+                    in1=source(h),
+                    op0=ALU.mult,
+                    op1=ALU.mult,
+                    accum_out=partial[i][:, j : j + 1],
+                )
+            else:
                 nc.scalar.activation(
                     out=squares[:],
-                    in_=source(t, j - (SQUARED - 1), SQUARED),
+                    in_=source(h),
                     func=ACT.Square,
-                    accum_out=partial[t][:, j // SQUARED : j // SQUARED + 1],
+                    accum_out=partial[i][:, j : j + 1],
                 )
 
-        def norm(t):
-            total = keep.tile([P, 1], F32, name="total%d" % t)
-            nc.vector.reduce_sum(out=total[:], in_=partial[t][:], axis=AXIS.X)
-            root = keep.tile([P, 1], F32, name="root%d" % t)
+        def norm(i):
+            total = keep.tile([P, 1], F32, name="total%d" % i)
+            nc.vector.reduce_sum(out=total[:], in_=partial[i][:], axis=AXIS.X)
+            root = keep.tile([P, 1], F32, name="root%d" % i)
             nc.scalar.activation(out=root[:], in_=total[:], func=ACT.Sqrt)
-            roots[t] = root
+            roots[i] = root
 
-        def factor(t):
-            scale = keep.tile([P, 1], F32, name="scale%d" % t)
-            factors[t] = scale
-            if t >= X_TILES:
-                nc.vector.reciprocal(out=scale[:], in_=roots[t][:])
+        def factor(i):
+            kind, t = SEQUENCE[i]
+            scale = keep.tile([P, 1], F32, name="scale%d" % i)
+            factors[i] = scale
+            if kind == "w":
+                nc.vector.reciprocal(out=scale[:], in_=roots[i][:])
                 return
             reach = keep.tile([P, 1], F32, name="reach%d" % t)
             nc.vector.reciprocal(out=reach[:], in_=distance[t][:])
@@ -147,7 +164,7 @@ def tile_metaembedding_classifier_pb_k_kernel(
             shrink = keep.tile([P, 1], F32, name="shrink%d" % t)
             nc.vector.tensor_scalar(
                 out=shrink[:],
-                in0=roots[t][:],
+                in0=roots[i][:],
                 scalar1=reach[:, 0:1],
                 scalar2=1.0,
                 op0=ALU.mult,
@@ -164,12 +181,11 @@ def tile_metaembedding_classifier_pb_k_kernel(
             )
 
         def scale_and_transpose(g):
-            t, j = divmod(g, CHUNKS)
-            scaled = stream.tile([P, CHUNK], BF16, tag="scaled", bufs=2)
+            scaled = stream.tile([P, CHUNK], BF16, tag="scaled")
             nc.vector.tensor_scalar(
                 out=scaled[:],
-                in0=source(t, j),
-                scalar1=factors[t][:, 0:1],
+                in0=source(g),
+                scalar1=factors[g // CHUNKS][:, 0:1],
                 scalar2=None,
                 op0=ALU.mult,
             )
@@ -186,8 +202,8 @@ def tile_metaembedding_classifier_pb_k_kernel(
                     )
                 banks[g].append(bank)
 
-        def empty_banks(g, by_vector):
-            ordered = stream.tile([P, CHUNK], BF16, tag="ordered", align_bytes=64)
+        def empty_banks(g, vector_banks):
+            ordered = stream.tile([P, CHUNK], BF16, tag="ordered", bufs=3, align_bytes=64)
             grouped[g] = ordered
             pairs = ordered[:].bitcast(F32)
             for n in range(CHUNK_BANKS):
@@ -195,55 +211,63 @@ def tile_metaembedding_classifier_pb_k_kernel(
                     "p (q r u) -> p q r u", r=P, u=2
                 )
                 src = banks[g][n][:].rearrange("p (q u r) -> p q r u", r=P, u=2)
-                if by_vector and not (n == 0 and g % RELIEF == 0):
+                if n < vector_banks:
                     nc.vector.tensor_copy(out=dst, in_=src)
                 else:
                     nc.scalar.copy(out=dst, in_=src)
 
         def quantise(g):
-            t, j = divmod(g, CHUNKS)
-            if t < X_TILES:
-                first = (t * PASSES + j * CHUNK_PASSES) * P
-                codes = x_codes[:, first : first + CHUNK_CODES]
-                scales = x_scales[:, first : first + CHUNK_CODES]
+            i, j = divmod(g, CHUNKS)
+            if SEQUENCE[i] in kept:
+                codes, scales = kept[SEQUENCE[i]]
+                cols = slice(j * CHUNK_CODES, (j + 1) * CHUNK_CODES)
+                operand[g] = (codes[:, cols], scales[:, cols])
             else:
-                w_codes = stream.tile([P, CHUNK_CODES], U32, tag="w_codes", align_bytes=64)
-                w_scales = stream.tile([P, CHUNK_CODES], U8, tag="w_scales", align_bytes=64)
-                w_operand[g] = (w_codes, w_scales)
-                codes = w_codes[:]
-                scales = w_scales[:]
+                codes = stream.tile([P, CHUNK_CODES], U32, tag="codes", align_bytes=64)
+                scales = stream.tile([P, CHUNK_CODES], U8, tag="scales", align_bytes=64)
+                operand[g] = (codes[:], scales[:])
+            codes, scales = operand[g]
             nc.vector.quantize_mx(out=codes.bitcast(FP8X4), scales=scales, in_=grouped[g][:])
 
         def multiply(g):
-            t, j = divmod(g, CHUNKS)
-            w_codes, w_scales = w_operand[g]
-            for s in range(X_TILES):
+            i, j = divmod(g, CHUNKS)
+            kind = SEQUENCE[i][0]
+            for m in range(i):
+                if SEQUENCE[m][0] == kind:
+                    continue
+                other = operand[m * CHUNKS + j]
+                x_side, w_side = (operand[g], other) if kind == "x" else (other, operand[g])
                 if j == 0:
-                    product = psum.tile([P, P], F32, tag="product", bufs=X_TILES)
-                    sums[(t, s)] = product
+                    product = psum.tile([P, P], F32, tag="product", bufs=2)
+                    sums[(i, m)] = product
                 for q in range(CHUNK_PASSES):
-                    k_pass = j * CHUNK_PASSES + q
-                    x_cols = slice((s * PASSES + k_pass) * P, (s * PASSES + k_pass + 1) * P)
-                    w_cols = slice(q * P, (q + 1) * P)
+                    cols = slice(q * P, (q + 1) * P)
                     nc.tensor.matmul_mx(
-                        out=sums[(t, s)][:],
-                        lhsT=x_codes[:, x_cols].bitcast(FP8X4),
-                        lhsT_scale=x_scales[:, x_cols],
-                        rhs=w_codes[:, w_cols].bitcast(FP8X4),
-                        rhs_scale=w_scales[:, w_cols],
-                        start=(k_pass == 0),
-                        stop=(k_pass == PASSES - 1),
+                        out=sums[(i, m)][:],
+                        lhsT=x_side[0][:, cols].bitcast(FP8X4),
+                        lhsT_scale=x_side[1][:, cols],
+                        rhs=w_side[0][:, cols].bitcast(FP8X4),
+                        rhs_scale=w_side[1][:, cols],
+                        start=(j == 0 and q == 0),
+                        stop=(j == CHUNKS - 1 and q == CHUNK_PASSES - 1),
                     )
 
-        def store(t):
-            cols = slice((t - X_TILES) * P, (t - X_TILES + 1) * P)
-            for s in range(X_TILES):
+        def store(i):
+            kind, t = SEQUENCE[i]
+            for m in range(i):
+                other_kind, s = SEQUENCE[m]
+                if other_kind == kind:
+                    continue
+                x_tile, w_tile = (t, s) if kind == "x" else (s, t)
                 logits = stream.tile([P, P], F32, tag="logits")
                 if s % 2 == 0:
-                    nc.vector.tensor_copy(out=logits[:], in_=sums[(t, s)][:])
+                    nc.vector.tensor_copy(out=logits[:], in_=sums[(i, m)][:])
                 else:
-                    nc.scalar.copy(out=logits[:], in_=sums[(t, s)][:])
-                nc.sync.dma_start(out=out[s * P : (s + 1) * P, cols], in_=logits[:])
+                    nc.scalar.copy(out=logits[:], in_=sums[(i, m)][:])
+                nc.sync.dma_start(
+                    out=out[x_tile * P : (x_tile + 1) * P, w_tile * P : (w_tile + 1) * P],
+                    in_=logits[:],
+                )
 
         for h in range(AHEAD):
             load(h)
@@ -260,10 +284,14 @@ def tile_metaembedding_classifier_pb_k_kernel(
             if 0 <= g < STEPS:
                 scale_and_transpose(g)
             if 0 <= g - 1 < STEPS:
-                empty_banks(g - 1, by_vector=(X_TILES * CHUNKS <= h < STEPS))
+                if kind_of(h) == "w":
+                    vector_banks = 2 if kind_of(g - 1) == "w" or g % 2 == 0 else 1
+                else:
+                    vector_banks = 0
+                empty_banks(g - 1, vector_banks)
             if 0 <= g - 2 < STEPS:
                 quantise(g - 2)
-            if (g - 3) % CHUNKS == CHUNKS - 1 and X_TILES * CHUNKS <= g - 3 < STEPS:
+            if (g - 3) % CHUNKS == CHUNKS - 1 and CHUNKS <= g - 3 < STEPS:
                 store((g - 3) // CHUNKS)
-            if X_TILES * CHUNKS <= g - 2 < STEPS:
+            if CHUNKS <= g - 2 < STEPS:
                 multiply(g - 2)

@@ -21,7 +21,7 @@ P = 128
 X_TILES = B // P
 W_TILES = C // P
 
-SEQUENCE = (("w", 0), ("x", 0), ("w", 1), ("x", 1), ("w", 2), ("w", 3))
+SEQUENCE = (("x", 0), ("w", 0), ("x", 1), ("w", 1), ("w", 2), ("w", 3))
 
 K_PASS = 4 * P
 PASSES = D // K_PASS
@@ -68,7 +68,7 @@ def tile_metaembedding_classifier_pb_k_kernel(
             distance[t] = dist
 
         kept = {}
-        for kind, t in SEQUENCE[:4]:
+        for kind, t in SEQUENCE[:3]:
             codes = keep.tile([P, PASSES * P], U32, name="codes_%s%d" % (kind, t), align_bytes=64)
             scales = keep.tile([P, PASSES * P], U8, name="scales_%s%d" % (kind, t), align_bytes=64)
             kept[(kind, t)] = (codes, scales)
@@ -77,6 +77,8 @@ def tile_metaembedding_classifier_pb_k_kernel(
         raw = {}
         slots = {}
         partial = {}
+        filled = {}
+        totals = {}
         roots = {}
         factors = {}
         banks = {}
@@ -111,11 +113,8 @@ def tile_metaembedding_classifier_pb_k_kernel(
                     slots[(i, j // W_SLOT_CHUNKS)] = weights
                 nc.sync.dma_start(out=source(h), in_=W_cos[rows, cols])
 
-        def sum_squares(h):
+        def add(h):
             i, j = divmod(h, CHUNKS)
-            if j == 0:
-                parts = keep.tile([P, CHUNKS], F32, name="parts%d" % i)
-                partial[i] = parts
             if SEQUENCE[i][0] == "x":
                 fused = ring.tile([P, CHUNK], F32, tag="slot")
                 slots[(i, j)] = fused
@@ -123,30 +122,42 @@ def tile_metaembedding_classifier_pb_k_kernel(
                 nc.vector.tensor_tensor(
                     out=fused[:], in0=direct[:], in1=infused[:], op=ALU.add
                 )
-            if i == 0 and j % 2 == 1:
+
+        def sum_squares(h, vector_columns):
+            i, j = divmod(h, CHUNKS)
+            if j == 0:
+                parts = keep.tile([P, 2 * CHUNKS], F32, name="parts%d" % i)
+                partial[i] = parts
+                filled[i] = 0
+            if vector_columns > 0:
                 unread = stream.tile([P, CHUNK], BF16, tag="scaled")
                 nc.vector.scalar_tensor_tensor(
-                    out=unread[:],
-                    in0=source(h),
+                    out=unread[:, 0:vector_columns],
+                    in0=source(h)[:, 0:vector_columns],
                     scalar=1.0,
-                    in1=source(h),
+                    in1=source(h)[:, 0:vector_columns],
                     op0=ALU.mult,
                     op1=ALU.mult,
-                    accum_out=partial[i][:, j : j + 1],
+                    accum_out=partial[i][:, filled[i] : filled[i] + 1],
                 )
-            else:
+                filled[i] += 1
+            if vector_columns < CHUNK:
                 nc.scalar.activation(
-                    out=squares[:],
-                    in_=source(h),
+                    out=squares[:, vector_columns:CHUNK],
+                    in_=source(h)[:, vector_columns:CHUNK],
                     func=ACT.Square,
-                    accum_out=partial[i][:, j : j + 1],
+                    accum_out=partial[i][:, filled[i] : filled[i] + 1],
                 )
+                filled[i] += 1
 
         def norm(i):
             total = keep.tile([P, 1], F32, name="total%d" % i)
-            nc.vector.reduce_sum(out=total[:], in_=partial[i][:], axis=AXIS.X)
+            nc.vector.reduce_sum(out=total[:], in_=partial[i][:, 0 : filled[i]], axis=AXIS.X)
+            totals[i] = total
+
+        def square_root(i):
             root = keep.tile([P, 1], F32, name="root%d" % i)
-            nc.scalar.activation(out=root[:], in_=total[:], func=ACT.Sqrt)
+            nc.scalar.activation(out=root[:], in_=totals[i][:], func=ACT.Sqrt)
             roots[i] = root
 
         def factor(i):
@@ -276,11 +287,9 @@ def tile_metaembedding_classifier_pb_k_kernel(
             if h + AHEAD < STEPS:
                 load(h + AHEAD)
             if h < STEPS:
-                sum_squares(h)
-            if h % CHUNKS == 0 and 0 < h <= STEPS:
-                norm(h // CHUNKS - 1)
+                add(h)
             if h % CHUNKS == 1 and 1 < h <= STEPS + 1:
-                factor(h // CHUNKS - 1)
+                square_root(h // CHUNKS - 1)
             if 0 <= g < STEPS:
                 scale_and_transpose(g)
             if 0 <= g - 1 < STEPS:
@@ -289,8 +298,14 @@ def tile_metaembedding_classifier_pb_k_kernel(
                 else:
                     vector_banks = 0
                 empty_banks(g - 1, vector_banks)
+            if h < STEPS:
+                sum_squares(h, CHUNK // 2 if g < 0 and kind_of(h) == "w" else 0)
             if 0 <= g - 2 < STEPS:
                 quantise(g - 2)
+            if h % CHUNKS == 0 and 0 < h <= STEPS:
+                norm(h // CHUNKS - 1)
+            if h % CHUNKS == 1 and 1 < h <= STEPS + 1:
+                factor(h // CHUNKS - 1)
             if (g - 3) % CHUNKS == CHUNKS - 1 and CHUNKS <= g - 3 < STEPS:
                 store((g - 3) // CHUNKS)
             if CHUNKS <= g - 2 < STEPS:

@@ -21,7 +21,7 @@ P = 128
 X_TILES = B // P
 W_TILES = C // P
 
-SEQUENCE = (("x", 0), ("w", 0), ("x", 1), ("w", 1), ("w", 2), ("w", 3))
+SEQUENCE = (("w", 0), ("x", 0), ("w", 1), ("x", 1), ("w", 2), ("w", 3))
 
 K_PASS = 4 * P
 PASSES = D // K_PASS
@@ -68,7 +68,7 @@ def tile_metaembedding_classifier_pb_k_kernel(
             distance[t] = dist
 
         kept = {}
-        for kind, t in SEQUENCE[:3]:
+        for kind, t in SEQUENCE[:4]:
             codes = keep.tile([P, PASSES * P], U32, name="codes_%s%d" % (kind, t), align_bytes=64)
             scales = keep.tile([P, PASSES * P], U8, name="scales_%s%d" % (kind, t), align_bytes=64)
             kept[(kind, t)] = (codes, scales)

@@ -36,7 +36,15 @@ CHUNK_BANKS = CHUNK // 2 // BANK_WORDS
 
 SLOT_BYTES = 4 * CHUNK
 W_SLOT_CHUNKS = 2
-RING_SLOTS = 12
+RING_SLOTS = 11
+
+GRAM_PLACE = 4
+GROUP = D // P
+GRAM = GROUP // 2
+GRAM_ROWS = 32
+GRAM_LOADS = range(12, 20, 2)
+GRAM_STEPS = range(22, 38)
+GRAM_STEP = GRAM // len(GRAM_STEPS)
 
 AHEAD = 2
 LEAD = 2
@@ -73,6 +81,8 @@ def tile_metaembedding_classifier_pb_k_kernel(
             scales = keep.tile([P, PASSES * P], U8, name="scales_%s%d" % (kind, t), align_bytes=64)
             kept[(kind, t)] = (codes, scales)
         squares = keep.tile([P, CHUNK], BF16)
+        by_feature = keep.tile([P, P, GRAM], BF16)
+        gram = psum.tile([P, P], F32, tag="gram", bufs=1)
 
         raw = {}
         slots = {}
@@ -113,6 +123,35 @@ def tile_metaembedding_classifier_pb_k_kernel(
                     slots[(i, j // W_SLOT_CHUNKS)] = weights
                 nc.sync.dma_start(out=source(h), in_=W_cos[rows, cols])
 
+        def load_gram(n):
+            t = SEQUENCE[GRAM_PLACE][1]
+            rows = slice(t * P + n * GRAM_ROWS, t * P + (n + 1) * GRAM_ROWS)
+            nc.sync.dma_start(
+                out=by_feature[:, n * GRAM_ROWS : (n + 1) * GRAM_ROWS, :],
+                in_=W_cos[rows, :].rearrange("r (p f) -> p r f", f=GROUP)[:, :, 0:GRAM],
+            )
+
+        def multiply_gram(n):
+            for f in range(n * GRAM_STEP, (n + 1) * GRAM_STEP):
+                nc.tensor.matmul(
+                    out=gram[:],
+                    lhsT=by_feature[:, :, f],
+                    rhs=by_feature[:, :, f],
+                    start=(f == 0),
+                    stop=(f == GRAM - 1),
+                )
+
+        def take_diagonal():
+            i = GRAM_PLACE
+            diagonal = keep.tile([P, P], F32)
+            nc.vector.tensor_tensor(
+                out=diagonal[:], in0=gram[:], in1=identity[:], op=ALU.mult
+            )
+            nc.vector.reduce_sum(
+                out=partial[i][:, filled[i] : filled[i] + 1], in_=diagonal[:], axis=AXIS.X
+            )
+            filled[i] += 1
+
         def add(h):
             i, j = divmod(h, CHUNKS)
             if SEQUENCE[i][0] == "x":
@@ -141,7 +180,15 @@ def tile_metaembedding_classifier_pb_k_kernel(
                     accum_out=partial[i][:, filled[i] : filled[i] + 1],
                 )
                 filled[i] += 1
-            if vector_columns < CHUNK:
+            if i == GRAM_PLACE:
+                nc.scalar.activation(
+                    out=squares[:, 0 : CHUNK // 2].rearrange("p (n f) -> p n f", f=GROUP - GRAM),
+                    in_=source(h).rearrange("p (n f) -> p n f", f=GROUP)[:, :, GRAM:GROUP],
+                    func=ACT.Square,
+                    accum_out=partial[i][:, filled[i] : filled[i] + 1],
+                )
+                filled[i] += 1
+            elif vector_columns < CHUNK:
                 nc.scalar.activation(
                     out=squares[:, vector_columns:CHUNK],
                     in_=source(h)[:, vector_columns:CHUNK],
@@ -203,7 +250,7 @@ def tile_metaembedding_classifier_pb_k_kernel(
             words = scaled[:].bitcast(F32)
             banks[g] = []
             for n in range(CHUNK_BANKS):
-                bank = psum.tile([P, BANK_WORDS], F32, tag="bank", bufs=6)
+                bank = psum.tile([P, BANK_WORDS], F32, tag="bank", bufs=5)
                 for b in range(BANK_BLOCKS):
                     block = n * BANK_BLOCKS + b
                     nc.tensor.transpose(
@@ -214,7 +261,7 @@ def tile_metaembedding_classifier_pb_k_kernel(
                 banks[g].append(bank)
 
         def empty_banks(g, vector_banks):
-            ordered = stream.tile([P, CHUNK], BF16, tag="ordered", bufs=3, align_bytes=64)
+            ordered = stream.tile([P, CHUNK], BF16, tag="ordered", bufs=2, align_bytes=64)
             grouped[g] = ordered
             pairs = ordered[:].bitcast(F32)
             for n in range(CHUNK_BANKS):
@@ -286,15 +333,24 @@ def tile_metaembedding_classifier_pb_k_kernel(
             g = h - CHUNKS - LEAD
             if h + AHEAD < STEPS:
                 load(h + AHEAD)
+            if h in GRAM_LOADS:
+                load_gram(GRAM_LOADS.index(h))
             if h < STEPS:
                 add(h)
             if h % CHUNKS == 1 and 1 < h <= STEPS + 1:
                 square_root(h // CHUNKS - 1)
             if 0 <= g < STEPS:
                 scale_and_transpose(g)
+            if h in GRAM_STEPS:
+                multiply_gram(GRAM_STEPS.index(h))
             if 0 <= g - 1 < STEPS:
                 if kind_of(h) == "w":
-                    vector_banks = 2 if kind_of(g - 1) == "w" or g % 2 == 0 else 1
+                    if h // CHUNKS == GRAM_PLACE:
+                        vector_banks = 1 if kind_of(g - 1) == "w" or g % 2 == 0 else 0
+                    elif kind_of(g - 1) == "w":
+                        vector_banks = 2
+                    else:
+                        vector_banks = 2 if g % 2 == 0 else 1
                 else:
                     vector_banks = 0
                 empty_banks(g - 1, vector_banks)
@@ -302,6 +358,8 @@ def tile_metaembedding_classifier_pb_k_kernel(
                 sum_squares(h, CHUNK // 2 if g < 0 and kind_of(h) == "w" else 0)
             if 0 <= g - 2 < STEPS:
                 quantise(g - 2)
+            if h == (GRAM_PLACE + 1) * CHUNKS - 1:
+                take_diagonal()
             if h % CHUNKS == 0 and 0 < h <= STEPS:
                 norm(h // CHUNKS - 1)
             if h % CHUNKS == 1 and 1 < h <= STEPS + 1:

@@ -75,11 +75,14 @@ def tile_metaembedding_classifier_pb_k_kernel(
             nc.scalar.dma_start(out=dist[:], in_=min_dist[t * P : (t + 1) * P, :])
             distance[t] = dist
 
+        shared = {}
         kept = {}
         for kind, t in SEQUENCE[:4]:
             codes = keep.tile([P, PASSES * P], U32, name="codes_%s%d" % (kind, t), align_bytes=64)
-            scales = keep.tile([P, PASSES * P], U8, name="scales_%s%d" % (kind, t), align_bytes=64)
-            kept[(kind, t)] = (codes, scales)
+            if t == 0:
+                planes = keep.tile([P, PASSES * P], U8, name="scales_%s" % kind, align_bytes=64)
+                shared[kind] = planes
+            kept[(kind, t)] = (codes, shared[kind][4 * t : P, :])
         squares = keep.tile([P, CHUNK], BF16)
         by_feature = keep.tile([P, P, GRAM], BF16)
         gram = psum.tile([P, P], F32, tag="gram", bufs=1)
@@ -169,7 +172,7 @@ def tile_metaembedding_classifier_pb_k_kernel(
                 partial[i] = parts
                 filled[i] = 0
             if vector_columns > 0:
-                unread = stream.tile([P, CHUNK], BF16, tag="scaled")
+                unread = stream.tile([P, CHUNK], BF16, tag="rounded")
                 nc.vector.scalar_tensor_tensor(
                     out=unread[:, 0:vector_columns],
                     in0=source(h)[:, 0:vector_columns],
@@ -239,15 +242,18 @@ def tile_metaembedding_classifier_pb_k_kernel(
             )
 
         def scale_and_transpose(g):
-            scaled = stream.tile([P, CHUNK], BF16, tag="scaled")
+            scaled = source(g)
+            if kind_of(g) == "x":
+                rounded = stream.tile([P, CHUNK], BF16, tag="rounded")
+                scaled = rounded[:]
             nc.vector.tensor_scalar(
-                out=scaled[:],
+                out=scaled,
                 in0=source(g),
                 scalar1=factors[g // CHUNKS][:, 0:1],
                 scalar2=None,
                 op0=ALU.mult,
             )
-            words = scaled[:].bitcast(F32)
+            words = scaled.bitcast(F32)
             banks[g] = []
             for n in range(CHUNK_BANKS):
                 bank = psum.tile([P, BANK_WORDS], F32, tag="bank", bufs=5)
@@ -261,7 +267,7 @@ def tile_metaembedding_classifier_pb_k_kernel(
                 banks[g].append(bank)
 
         def empty_banks(g, vector_banks):
-            ordered = stream.tile([P, CHUNK], BF16, tag="ordered", bufs=2, align_bytes=64)
+            ordered = stream.tile([P, CHUNK], BF16, tag="ordered", bufs=3, align_bytes=64)
             grouped[g] = ordered
             pairs = ordered[:].bitcast(F32)
             for n in range(CHUNK_BANKS):
@@ -317,7 +323,7 @@ def tile_metaembedding_classifier_pb_k_kernel(
                 if other_kind == kind:
                     continue
                 x_tile, w_tile = (t, s) if kind == "x" else (s, t)
-                logits = stream.tile([P, P], F32, tag="logits")
+                logits = stream.tile([P, P], F32, tag="logits", bufs=4)
                 if s % 2 == 0:
                     nc.vector.tensor_copy(out=logits[:], in_=sums[(i, m)][:])
                 else:

from contextlib import ExitStack

import concourse.mybir as mybir
from concourse.masks import make_identity

F32 = mybir.dt.float32
BF16 = mybir.dt.bfloat16
U32 = mybir.dt.uint32
U8 = mybir.dt.uint8
FP8X4 = mybir.dt.float8_e4m3fn_x4
ACT = mybir.ActivationFunctionType
ALU = mybir.AluOpType
AXIS = mybir.AxisListType

B, D, C = 256, 16384, 512
REACH_SCALE = 10.0
COS_SCALE = 16.0
FLOPS = 2 * B * C * D

P = 128
X_TILES = B // P
W_TILES = C // P

SEQUENCE = (("w", 0), ("x", 0), ("w", 1), ("x", 1), ("w", 2), ("w", 3))

K_PASS = 4 * P
PASSES = D // K_PASS
CHUNK = 2048
CHUNKS = D // CHUNK
STEPS = len(SEQUENCE) * CHUNKS
CHUNK_PASSES = CHUNK // K_PASS
CHUNK_CODES = CHUNK // 4
BANK_WORDS = 512
BANK_BLOCKS = BANK_WORDS // P
CHUNK_BANKS = CHUNK // 2 // BANK_WORDS

SLOT_BYTES = 4 * CHUNK
W_SLOT_CHUNKS = 2
RING_SLOTS = 11

GRAM_PLACE = 4
GROUP = D // P
GRAM = GROUP // 2
GRAM_ROWS = 32
GRAM_LOADS = range(12, 20, 2)
GRAM_STEPS = range(22, 38)
GRAM_STEP = GRAM // len(GRAM_STEPS)

AHEAD = 2
LEAD = 2


def tile_metaembedding_classifier_pb_k_kernel(
    tc, x, infused_feature, min_dist, W_cos, out
):
    nc = tc.nc
    with ExitStack() as ctx:
        ctx.enter_context(tc.manual_schedule())
        keep = ctx.enter_context(tc.tile_pool(name="keep", bufs=1))
        ring = ctx.enter_context(tc.tile_pool(name="ring", bufs=RING_SLOTS))
        stream = ctx.enter_context(tc.tile_pool(name="stream", bufs=2))
        psum = ctx.enter_context(tc.psum_pool(name="psum", bufs=1))

        identity = keep.tile([P, P], F32)
        make_identity(nc, identity[:])

        one = keep.tile([P, 1], F32)
        nc.vector.memset(one[:], 1.0)
        warm = keep.tile([P, 1], F32)
        nc.scalar.activation(out=warm[:], in_=one[:], func=ACT.Sqrt)

        distance = {}
        for t in range(X_TILES):
            dist = keep.tile([P, 1], BF16, name="dist%d" % t)
            nc.scalar.dma_start(out=dist[:], in_=min_dist[t * P : (t + 1) * P, :])
            distance[t] = dist

        shared = {}
        kept = {}
        for kind, t in SEQUENCE[:4]:
            codes = keep.tile([P, PASSES * P], U32, name="codes_%s%d" % (kind, t), align_bytes=64)
            if t == 0:
                planes = keep.tile([P, PASSES * P], U8, name="scales_%s" % kind, align_bytes=64)
                shared[kind] = planes
            kept[(kind, t)] = (codes, shared[kind][4 * t : P, :])
        squares = keep.tile([P, CHUNK], BF16)
        by_feature = keep.tile([P, P, GRAM], BF16)
        gram = psum.tile([P, P], F32, tag="gram", bufs=1)

        raw = {}
        slots = {}
        partial = {}
        filled = {}
        totals = {}
        roots = {}
        factors = {}
        banks = {}
        grouped = {}
        operand = {}
        sums = {}

        def kind_of(h):
            return SEQUENCE[h // CHUNKS][0] if 0 <= h < STEPS else None

        def source(h):
            i, j = divmod(h, CHUNKS)
            if SEQUENCE[i][0] == "x":
                return slots[(i, j)][:]
            c = (j % W_SLOT_CHUNKS) * CHUNK
            return slots[(i, j // W_SLOT_CHUNKS)][:, c : c + CHUNK]

        def load(h):
            i, j = divmod(h, CHUNKS)
            kind, t = SEQUENCE[i]
            rows = slice(t * P, (t + 1) * P)
            cols = slice(j * CHUNK, (j + 1) * CHUNK)
            if kind == "x":
                direct = stream.tile([P, CHUNK], BF16, tag="direct", bufs=AHEAD + 1)
                nc.sync.dma_start(out=direct[:], in_=x[rows, cols])
                infused = stream.tile([P, CHUNK], BF16, tag="infused", bufs=AHEAD + 1)
                nc.sync.dma_start(out=infused[:], in_=infused_feature[rows, cols])
                raw[h] = (direct, infused)
            else:
                if j % W_SLOT_CHUNKS == 0:
                    weights = ring.tile([P, W_SLOT_CHUNKS * CHUNK], BF16, tag="slot")
                    slots[(i, j // W_SLOT_CHUNKS)] = weights
                nc.sync.dma_start(out=source(h), in_=W_cos[rows, cols])

        def load_gram(n):
            t = SEQUENCE[GRAM_PLACE][1]
            rows = slice(t * P + n * GRAM_ROWS, t * P + (n + 1) * GRAM_ROWS)
            nc.sync.dma_start(
                out=by_feature[:, n * GRAM_ROWS : (n + 1) * GRAM_ROWS, :],
                in_=W_cos[rows, :].rearrange("r (p f) -> p r f", f=GROUP)[:, :, 0:GRAM],
            )

        def multiply_gram(n):
            for f in range(n * GRAM_STEP, (n + 1) * GRAM_STEP):
                nc.tensor.matmul(
                    out=gram[:],
                    lhsT=by_feature[:, :, f],
                    rhs=by_feature[:, :, f],
                    start=(f == 0),
                    stop=(f == GRAM - 1),
                )

        def take_diagonal():
            i = GRAM_PLACE
            diagonal = keep.tile([P, P], F32)
            nc.vector.tensor_tensor(
                out=diagonal[:], in0=gram[:], in1=identity[:], op=ALU.mult
            )
            nc.vector.reduce_sum(
                out=partial[i][:, filled[i] : filled[i] + 1], in_=diagonal[:], axis=AXIS.X
            )
            filled[i] += 1

        def add(h):
            i, j = divmod(h, CHUNKS)
            if SEQUENCE[i][0] == "x":
                fused = ring.tile([P, CHUNK], F32, tag="slot")
                slots[(i, j)] = fused
                direct, infused = raw[h]
                nc.vector.tensor_tensor(
                    out=fused[:], in0=direct[:], in1=infused[:], op=ALU.add
                )

        def sum_squares(h, vector_columns):
            i, j = divmod(h, CHUNKS)
            if j == 0:
                parts = keep.tile([P, 2 * CHUNKS], F32, name="parts%d" % i)
                partial[i] = parts
                filled[i] = 0
            if vector_columns > 0:
                unread = stream.tile([P, CHUNK], BF16, tag="rounded")
                nc.vector.scalar_tensor_tensor(
                    out=unread[:, 0:vector_columns],
                    in0=source(h)[:, 0:vector_columns],
                    scalar=1.0,
                    in1=source(h)[:, 0:vector_columns],
                    op0=ALU.mult,
                    op1=ALU.mult,
                    accum_out=partial[i][:, filled[i] : filled[i] + 1],
                )
                filled[i] += 1
            if i == GRAM_PLACE:
                nc.scalar.activation(
                    out=squares[:, 0 : CHUNK // 2].rearrange("p (n f) -> p n f", f=GROUP - GRAM),
                    in_=source(h).rearrange("p (n f) -> p n f", f=GROUP)[:, :, GRAM:GROUP],
                    func=ACT.Square,
                    accum_out=partial[i][:, filled[i] : filled[i] + 1],
                )
                filled[i] += 1
            elif vector_columns < CHUNK:
                nc.scalar.activation(
                    out=squares[:, vector_columns:CHUNK],
                    in_=source(h)[:, vector_columns:CHUNK],
                    func=ACT.Square,
                    accum_out=partial[i][:, filled[i] : filled[i] + 1],
                )
                filled[i] += 1

        def norm(i):
            total = keep.tile([P, 1], F32, name="total%d" % i)
            nc.vector.reduce_sum(out=total[:], in_=partial[i][:, 0 : filled[i]], axis=AXIS.X)
            totals[i] = total

        def square_root(i):
            root = keep.tile([P, 1], F32, name="root%d" % i)
            nc.scalar.activation(out=root[:], in_=totals[i][:], func=ACT.Sqrt)
            roots[i] = root

        def factor(i):
            kind, t = SEQUENCE[i]
            scale = keep.tile([P, 1], F32, name="scale%d" % i)
            factors[i] = scale
            if kind == "w":
                nc.vector.reciprocal(out=scale[:], in_=roots[i][:])
                return
            reach = keep.tile([P, 1], F32, name="reach%d" % t)
            nc.vector.reciprocal(out=reach[:], in_=distance[t][:])
            nc.vector.tensor_scalar(
                out=reach[:], in0=reach[:], scalar1=REACH_SCALE, scalar2=None, op0=ALU.mult
            )
            shrink = keep.tile([P, 1], F32, name="shrink%d" % t)
            nc.vector.tensor_scalar(
                out=shrink[:],
                in0=roots[i][:],
                scalar1=reach[:, 0:1],
                scalar2=1.0,
                op0=ALU.mult,
                op1=ALU.add,
            )
            nc.vector.reciprocal(out=shrink[:], in_=shrink[:])
            nc.vector.tensor_scalar(
                out=scale[:],
                in0=shrink[:],
                scalar1=reach[:, 0:1],
                scalar2=COS_SCALE,
                op0=ALU.mult,
                op1=ALU.mult,
            )

        def scale_and_transpose(g):
            scaled = source(g)
            if kind_of(g) == "x":
                rounded = stream.tile([P, CHUNK], BF16, tag="rounded")
                scaled = rounded[:]
            nc.vector.tensor_scalar(
                out=scaled,
                in0=source(g),
                scalar1=factors[g // CHUNKS][:, 0:1],
                scalar2=None,
                op0=ALU.mult,
            )
            words = scaled.bitcast(F32)
            banks[g] = []
            for n in range(CHUNK_BANKS):
                bank = psum.tile([P, BANK_WORDS], F32, tag="bank", bufs=5)
                for b in range(BANK_BLOCKS):
                    block = n * BANK_BLOCKS + b
                    nc.tensor.transpose(
                        out=bank[:, b * P : (b + 1) * P],
                        in_=words[:, block * P : (block + 1) * P],
                        identity=identity[:],
                    )
                banks[g].append(bank)

        def empty_banks(g, vector_banks):
            ordered = stream.tile([P, CHUNK], BF16, tag="ordered", bufs=3, align_bytes=64)
            grouped[g] = ordered
            pairs = ordered[:].bitcast(F32)
            for n in range(CHUNK_BANKS):
                dst = pairs[:, n * BANK_WORDS : (n + 1) * BANK_WORDS].rearrange(
                    "p (q r u) -> p q r u", r=P, u=2
                )
                src = banks[g][n][:].rearrange("p (q u r) -> p q r u", r=P, u=2)
                if n < vector_banks:
                    nc.vector.tensor_copy(out=dst, in_=src)
                else:
                    nc.scalar.copy(out=dst, in_=src)

        def quantise(g):
            i, j = divmod(g, CHUNKS)
            if SEQUENCE[i] in kept:
                codes, scales = kept[SEQUENCE[i]]
                cols = slice(j * CHUNK_CODES, (j + 1) * CHUNK_CODES)
                operand[g] = (codes[:, cols], scales[:, cols])
            else:
                codes = stream.tile([P, CHUNK_CODES], U32, tag="codes", align_bytes=64)
                scales = stream.tile([P, CHUNK_CODES], U8, tag="scales", align_bytes=64)
                operand[g] = (codes[:], scales[:])
            codes, scales = operand[g]
            nc.vector.quantize_mx(out=codes.bitcast(FP8X4), scales=scales, in_=grouped[g][:])

        def multiply(g):
            i, j = divmod(g, CHUNKS)
            kind = SEQUENCE[i][0]
            for m in range(i):
                if SEQUENCE[m][0] == kind:
                    continue
                other = operand[m * CHUNKS + j]
                x_side, w_side = (operand[g], other) if kind == "x" else (other, operand[g])
                if j == 0:
                    product = psum.tile([P, P], F32, tag="product", bufs=2)
                    sums[(i, m)] = product
                for q in range(CHUNK_PASSES):
                    cols = slice(q * P, (q + 1) * P)
                    nc.tensor.matmul_mx(
                        out=sums[(i, m)][:],
                        lhsT=x_side[0][:, cols].bitcast(FP8X4),
                        lhsT_scale=x_side[1][:, cols],
                        rhs=w_side[0][:, cols].bitcast(FP8X4),
                        rhs_scale=w_side[1][:, cols],
                        start=(j == 0 and q == 0),
                        stop=(j == CHUNKS - 1 and q == CHUNK_PASSES - 1),
                    )

        def store(i):
            kind, t = SEQUENCE[i]
            for m in range(i):
                other_kind, s = SEQUENCE[m]
                if other_kind == kind:
                    continue
                x_tile, w_tile = (t, s) if kind == "x" else (s, t)
                logits = stream.tile([P, P], F32, tag="logits", bufs=4)
                if s % 2 == 0:
                    nc.vector.tensor_copy(out=logits[:], in_=sums[(i, m)][:])
                else:
                    nc.scalar.copy(out=logits[:], in_=sums[(i, m)][:])
                nc.sync.dma_start(
                    out=out[x_tile * P : (x_tile + 1) * P, w_tile * P : (w_tile + 1) * P],
                    in_=logits[:],
                )

        for h in range(AHEAD):
            load(h)
        for h in range(STEPS + CHUNKS + LEAD + 3):
            g = h - CHUNKS - LEAD
            if h + AHEAD < STEPS:
                load(h + AHEAD)
            if h in GRAM_LOADS:
                load_gram(GRAM_LOADS.index(h))
            if h < STEPS:
                add(h)
            if h % CHUNKS == 1 and 1 < h <= STEPS + 1:
                square_root(h // CHUNKS - 1)
            if 0 <= g < STEPS:
                scale_and_transpose(g)
            if h in GRAM_STEPS:
                multiply_gram(GRAM_STEPS.index(h))
            if 0 <= g - 1 < STEPS:
                if kind_of(h) == "w":
                    if h // CHUNKS == GRAM_PLACE:
                        vector_banks = 1 if kind_of(g - 1) == "w" or g % 2 == 0 else 0
                    elif kind_of(g - 1) == "w":
                        vector_banks = 2
                    else:
                        vector_banks = 2 if g % 2 == 0 else 1
                else:
                    vector_banks = 0
                empty_banks(g - 1, vector_banks)
            if h < STEPS:
                sum_squares(h, CHUNK // 2 if g < 0 and kind_of(h) == "w" else 0)
            if 0 <= g - 2 < STEPS:
                quantise(g - 2)
            if h == (GRAM_PLACE + 1) * CHUNKS - 1:
                take_diagonal()
            if h % CHUNKS == 0 and 0 < h <= STEPS:
                norm(h // CHUNKS - 1)
            if h % CHUNKS == 1 and 1 < h <= STEPS + 1:
                factor(h // CHUNKS - 1)
            if (g - 3) % CHUNKS == CHUNKS - 1 and CHUNKS <= g - 3 < STEPS:
                store((g - 3) // CHUNKS)
            if CHUNKS <= g - 2 < STEPS:
                multiply(g - 2)
